import numpy as np
import ml_dtypes


def mxq(x, axis, fmt="e4m3"):
    dtype, down = {"e4m3": (ml_dtypes.float8_e4m3fn, 7), "e5m2": (ml_dtypes.float8_e5m2, 14)}[fmt]
    v = np.moveaxis(np.asarray(x, np.float32).astype(ml_dtypes.bfloat16).astype(np.float64), axis, -1)
    blocks = v.reshape(v.shape[:-1] + (-1, 32))
    amax = np.abs(blocks).max(-1, keepdims=True)
    byte = np.maximum(np.where(amax > 0, np.frexp(amax)[1] - 1 + 127, 0) - down, 1)
    scale = np.exp2(byte - 127.0)
    codes = (blocks / scale).astype(np.float32).astype(dtype).astype(np.float64)
    return np.moveaxis((codes * scale).reshape(v.shape), -1, axis)


WIDE = False


def mx_kscale(k):
    if not WIDE:
        return np.ones(k)
    levels = np.array([10, -10, 5, -5, 0])
    if k % 512:
        return np.exp2(np.random.permutation(np.resize(levels, k // 32))).repeat(32)
    a = np.empty((k // 512, 16))
    for p in range(k // 512):
        a[p, :8] = np.random.permutation(np.resize(levels, 8))
        for g in range(8):
            far = levels[np.abs(levels - a[p, g]) >= 10]
            a[p, g + 8] = far[np.random.randint(len(far))]
    return np.exp2(a.ravel()).repeat(32)


BF16 = ml_dtypes.bfloat16


def bf(x):
    return np.asarray(x, np.float32).astype(BF16)


def f64(x):
    return np.asarray(x).astype(np.float64)


B, N, D, F1, F2, F3, G1, G2 = 4, 32, 512, 512, 1024, 512, 512, 512
ALPHA = 0.2


def lrelu(v):
    return np.maximum(v, ALPHA * v)


def setup_inputs():
    s, t = mx_kscale(F2), mx_kscale(F3 + D)
    return {"e2": bf(lrelu(np.random.standard_normal((B, N, N, F2))) * s),
            "x": bf(np.random.standard_normal((B, N, D)) * t[F3:]),
            "fe_w2": bf(np.random.standard_normal((F2, F3)) * (12.0 / N) / np.sqrt(F2) / s[:, None] * t[:F3]),
            "fe_b2": bf(np.random.standard_normal(F3) * (3.0 / N) * t[:F3]),
            "fn_w0": bf(np.random.standard_normal((F3 + D, G1)) * 0.25 / np.sqrt(F3 + D) / t[:, None]),
            "fn_b0": bf(np.random.standard_normal(G1) * 0.3)}


def reference(e2, x, fe_w2, fe_b2, fn_w0, fn_b0):
    a3 = lrelu((mxq(f64(e2), 3, "e4m3") @ mxq(f64(fe_w2), 0, "e4m3")) + f64(fe_b2))
    agg = a3.sum(axis=2)
    h = np.concatenate([agg, f64(x)], axis=-1)
    return lrelu((mxq(h, 2, "e4m3") @ mxq(f64(fn_w0), 0, "e4m3")) + f64(fn_b0))

@@ -1,0 +1,312 @@
+from contextlib import ExitStack
+
+import concourse.mybir as mybir
+from concourse.masks import make_identity
+
+F32 = mybir.dt.float32
+BF16 = mybir.dt.bfloat16
+U32 = mybir.dt.uint32
+U8 = mybir.dt.uint8
+FP8X4 = mybir.dt.float8_e4m3fn_x4
+ALU = mybir.AluOpType
+ACT = mybir.ActivationFunctionType
+AXIS = mybir.AxisListType
+
+P = 128
+PACK = 4
+K_PASS = P * PACK
+NODES = 128
+NEIGHBOURS = 32
+K = 1024
+PASSES = K // K_PASS
+WIDTH = 512
+F_TILES = WIDTH // P
+J_CHUNK = 4
+CHUNKS = NEIGHBOURS // J_CHUNK
+COLS = J_CHUNK * NODES
+WORD_BLOCKS = K // 2 // P
+ALPHA = 0.2
+GPSIMD_TILES = (0, 1)
+TENSOR_TILES = (2,)
+VECTOR_TILES = (3,)
+PSUM_BANKS = 8
+AGG_PASS, X_PASS = 0, 1
+
+FLOPS = 2 * NODES * NEIGHBOURS * K * WIDTH + 2 * NODES * K * WIDTH
+
+
+def regroup(copy, raw, grouped, g):
+    copy(
+        out=grouped[g][:].rearrange("p (c i t) -> p c t i", i=4, t=PACK),
+        in_=raw[:, g * PACK : (g + 1) * PACK, :].rearrange("p t (c i) -> p c t i", i=4),
+    )
+
+
+def regroup_by_tile(copy, raw, grouped, g):
+    copy(
+        out=grouped[g][:].rearrange("p (i m t) -> p i m t", i=F_TILES, t=PACK),
+        in_=raw[:, g * PACK : (g + 1) * PACK, :].rearrange("p t (m i) -> p i m t", i=F_TILES),
+    )
+
+
+def tile_graph_gan_pb_kernel(tc, e2, x, fe_w2, fe_b2, fn_w0, fn_b0, out):
+    nc = tc.nc
+    with ExitStack() as stack:
+        stack.enter_context(tc.manual_schedule())
+        keep = stack.enter_context(tc.tile_pool(name="keep", bufs=1))
+        stage = stack.enter_context(tc.tile_pool(name="stage", bufs=3))
+        work = stack.enter_context(tc.tile_pool(name="work", bufs=4))
+        psum_keep = stack.enter_context(tc.psum_pool(name="psum_keep", bufs=len(TENSOR_TILES)))
+        banks = stack.enter_context(
+            tc.psum_pool(name="banks", bufs=PSUM_BANKS - len(TENSOR_TILES))
+        )
+
+        ident_f32 = keep.tile([P, P], F32)
+        make_identity(nc, ident_f32[:])
+
+        x_sb = keep.tile([P, K_PASS], BF16)
+        nc.sync.dma_start(out=x_sb[:], in_=x.rearrange("b i d -> (b i) d"))
+        b2_raw = keep.tile([P, F_TILES], BF16)
+        nc.sync.dma_start(out=b2_raw[:], in_=fe_b2.rearrange("(p t) -> p t", p=P))
+        w1_raw = keep.tile([P, PASSES * PACK, WIDTH], BF16)
+        nc.sync.dma_start(
+            out=w1_raw[:].rearrange("p (g t) c -> p g t c", t=PACK),
+            in_=fe_w2.rearrange("(g p t) c -> p g t c", p=P, t=PACK),
+        )
+        e2_rows = e2.rearrange("b i j k -> (b i) (j k)")
+        e2_sb = []
+        for c in range(CHUNKS):
+            e2_c = keep.tile([P, J_CHUNK * K], BF16, name="e2_%d" % c)
+            pieces = max(1, J_CHUNK >> c)
+            run = J_CHUNK * K // pieces
+            for i in range(pieces):
+                first = c * J_CHUNK * K + i * run
+                nc.sync.dma_start(
+                    out=e2_c[:, i * run : (i + 1) * run], in_=e2_rows[:, first : first + run]
+                )
+            e2_sb.append(e2_c)
+        w0_raw = keep.tile([P, PASSES * PACK, WIDTH], BF16)
+        nc.sync.dma_start(
+            out=w0_raw[:].rearrange("p (g t) c -> p g t c", t=PACK),
+            in_=fn_w0.rearrange("(g p t) c -> p g t c", p=P, t=PACK),
+        )
+        b0_all = keep.tile([P, WIDTH], BF16)
+        nc.sync.dma_start(out=b0_all[:], in_=fn_b0.partition_broadcast(P))
+
+        h_grouped = keep.tile([P, PASSES * NODES * PACK], BF16, align_bytes=64)
+        h_view = h_grouped[:].rearrange("p (g n t) -> p g n t", g=PASSES, t=PACK)
+        h_codes = keep.tile([P, PASSES, NODES], U32, align_bytes=64)
+        h_scales = keep.tile([P, PASSES, NODES], U8, align_bytes=64)
+
+        def quantise_h(g):
+            nc.vector.quantize_mx(
+                out=h_codes[:, g, :].bitcast(FP8X4),
+                scales=h_scales[:, g, :],
+                in_=h_grouped[:, g * NODES * PACK : (g + 1) * NODES * PACK],
+            )
+
+        x_words = x_sb[:].bitcast(F32)
+        x_ps = banks.tile([P, 2, NODES], F32, tag="bank")
+        for u in range(2):
+            nc.tensor.transpose(x_ps[:, u, :], x_words[:, u::2], ident_f32[:])
+        nc.vector.tensor_copy(
+            out=h_grouped[:].bitcast(F32).rearrange("p (g n u) -> p g n u", g=PASSES, u=2)[
+                :, X_PASS, :, :
+            ],
+            in_=x_ps[:].rearrange("p u n -> p n u"),
+        )
+        quantise_h(X_PASS)
+
+        b2 = keep.tile([P, F_TILES], F32)
+        nc.vector.tensor_copy(out=b2[:], in_=b2_raw[:])
+        b2_alpha = keep.tile([P, F_TILES], F32)
+        nc.vector.tensor_scalar_mul(out=b2_alpha[:], in0=b2[:], scalar1=ALPHA)
+        b2_neg = keep.tile([P, F_TILES], F32)
+        nc.vector.tensor_scalar_mul(out=b2_neg[:], in0=b2[:], scalar1=-1.0)
+        b2_column = keep.tile([P, F_TILES], F32)
+        nc.vector.tensor_scalar_mul(out=b2_column[:], in0=b2[:], scalar1=float(CHUNKS))
+
+        def weight_tiles(name):
+            grouped = [
+                keep.tile([P, WIDTH * PACK], BF16, align_bytes=64, name="%s_grouped_%d" % (name, g))
+                for g in range(PASSES)
+            ]
+            codes = keep.tile([P, PASSES, WIDTH], U32, align_bytes=64, name="%s_codes" % name)
+            scales = keep.tile([P, PASSES, WIDTH], U8, align_bytes=64, name="%s_scales" % name)
+            return grouped, codes, scales
+
+        def quantise_weight(grouped, codes, scales):
+            for g in range(PASSES):
+                nc.vector.quantize_mx(
+                    out=codes[:, g, :].bitcast(FP8X4), scales=scales[:, g, :], in_=grouped[g][:]
+                )
+
+        w1_grouped, w1_codes, w1_scales = weight_tiles("w1")
+        for g in range(PASSES):
+            regroup_by_tile(nc.vector.tensor_copy, w1_raw, w1_grouped, g)
+        quantise_weight(w1_grouped, w1_codes, w1_scales)
+        w0_grouped, w0_codes, w0_scales = weight_tiles("w0")
+
+        def quantise_chunk(c):
+            e2_words = e2_sb[c][:].bitcast(F32)
+            grouped = stage.tile([P, PASSES * COLS * PACK], BF16, align_bytes=64)
+            grouped_words = grouped[:].bitcast(F32).rearrange(
+                "p (g j n u) -> p g j n u", g=PASSES, j=J_CHUNK, u=2
+            )
+            for j in range(J_CHUNK):
+                xt = banks.tile([P, WORD_BLOCKS, NODES], F32, tag="bank")
+                for w in range(WORD_BLOCKS):
+                    g, u = divmod(w, 2)
+                    first = (j * PASSES + g) * 2 * P
+                    nc.tensor.transpose(
+                        xt[:, w, :], e2_words[:, first + u : first + 2 * P : 2], ident_f32[:]
+                    )
+                nc.scalar.copy(
+                    out=grouped_words[:, :, j, :, :],
+                    in_=xt[:].rearrange("p (g u) n -> p g n u", u=2),
+                )
+            codes = stage.tile([P, PASSES, COLS], U32, align_bytes=64)
+            scales = stage.tile([P, PASSES, COLS], U8, align_bytes=64)
+            nc.vector.quantize_mx(
+                out=codes[:].rearrange("p g c -> p (g c)").bitcast(FP8X4),
+                scales=scales[:].rearrange("p g c -> p (g c)"),
+                in_=grouped[:],
+            )
+            return codes, scales
+
+        a3_sum = dict((t, keep.tile([P, COLS], F32, name="a3_sum_%d" % t)) for t in GPSIMD_TILES)
+        clip_sum = dict(
+            (t, keep.tile([P, COLS], F32, name="clip_sum_%d" % t))
+            for t in TENSOR_TILES + VECTOR_TILES
+        )
+        line_sum = dict(
+            (t, keep.tile([P, COLS], F32, name="line_sum_%d" % t))
+            for t in TENSOR_TILES + VECTOR_TILES
+        )
+        v_sum = dict((t, psum_keep.tile([P, COLS], F32, name="v_sum_%d" % t)) for t in TENSOR_TILES)
+
+        def edge_layer(c, codes, scales):
+            def multiply(bank, t, g, start, stop):
+                f_cols = slice(t * P, (t + 1) * P)
+                nc.tensor.matmul_mx(
+                    out=bank[:],
+                    lhsT=w1_codes[:, g, f_cols].bitcast(FP8X4),
+                    lhsT_scale=w1_scales[:, g, f_cols],
+                    rhs=codes[:, g, :].bitcast(FP8X4),
+                    rhs_scale=scales[:, g, :],
+                    start=start,
+                    stop=stop,
+                )
+
+            for t in range(F_TILES):
+                if t in TENSOR_TILES:
+                    for g in range(PASSES):
+                        multiply(
+                            v_sum[t], t, g, c == 0 and g == 0, c == CHUNKS - 1 and g == PASSES - 1
+                        )
+                acc = banks.tile([P, COLS], F32, tag="bank")
+                for g in range(PASSES):
+                    multiply(acc, t, g, g == 0, g == PASSES - 1)
+                if t in GPSIMD_TILES:
+                    scaled = work.tile([P, COLS], F32)
+                    nc.scalar.activation(
+                        out=scaled[:], in_=acc[:], func=ACT.Identity,
+                        bias=b2_alpha[:, t : t + 1], scale=ALPHA,
+                    )
+                    a3 = a3_sum[t] if c == 0 else work.tile([P, COLS], F32, name="a3")
+                    nc.vector.scalar_tensor_tensor(
+                        out=a3[:], in0=acc[:], scalar=b2[:, t : t + 1], in1=scaled[:],
+                        op0=ALU.add, op1=ALU.max,
+                    )
+                    if c > 0:
+                        nc.gpsimd.tensor_tensor(
+                            out=a3_sum[t][:], in0=a3_sum[t][:], in1=a3[:], op=ALU.add
+                        )
+                    continue
+                if t in VECTOR_TILES:
+                    if c == 0:
+                        nc.vector.tensor_scalar(
+                            out=line_sum[t][:], in0=acc[:], scalar1=ALPHA,
+                            scalar2=b2_column[:, t : t + 1], op0=ALU.mult, op1=ALU.add,
+                        )
+                    else:
+                        nc.vector.scalar_tensor_tensor(
+                            out=line_sum[t][:], in0=acc[:], scalar=ALPHA, in1=line_sum[t][:],
+                            op0=ALU.mult, op1=ALU.add,
+                        )
+                if c == 0:
+                    nc.vector.tensor_scalar_max(
+                        out=clip_sum[t][:], in0=acc[:], scalar1=b2_neg[:, t : t + 1]
+                    )
+                else:
+                    nc.vector.scalar_tensor_tensor(
+                        out=clip_sum[t][:], in0=acc[:], scalar=b2_neg[:, t : t + 1],
+                        in1=clip_sum[t][:], op0=ALU.max, op1=ALU.add,
+                    )
+
+        ready = quantise_chunk(0)
+        for c in range(CHUNKS):
+            following = quantise_chunk(c + 1) if c + 1 < CHUNKS else None
+            edge_layer(c, ready[0], ready[1])
+            ready = following
+            g = c - (CHUNKS - PASSES)
+            if g >= 0:
+                regroup(nc.scalar.copy, w0_raw, w0_grouped, g)
+        for t in TENSOR_TILES:
+            nc.scalar.activation(
+                out=line_sum[t][:], in_=v_sum[t][:], func=ACT.Identity,
+                bias=b2_column[:, t : t + 1], scale=ALPHA,
+            )
+        quantise_weight(w0_grouped, w0_codes, w0_scales)
+
+        out_ps = banks.tile([P, WIDTH], F32, tag="bank")
+
+        def node_layer(g, start, stop):
+            nc.tensor.matmul_mx(
+                out=out_ps[:],
+                lhsT=h_codes[:, g, :].bitcast(FP8X4),
+                lhsT_scale=h_scales[:, g, :],
+                rhs=w0_codes[:, g, :].bitcast(FP8X4),
+                rhs_scale=w0_scales[:, g, :],
+                start=start,
+                stop=stop,
+            )
+
+        node_layer(X_PASS, True, False)
+
+        def join_sums(t):
+            both = work.tile([P, COLS], F32)
+            nc.vector.scalar_tensor_tensor(
+                out=both[:], in0=clip_sum[t][:], scalar=1.0 - ALPHA, in1=line_sum[t][:],
+                op0=ALU.mult, op1=ALU.add,
+            )
+            return both
+
+        a3_cols = dict(
+            [(t, join_sums(t)) for t in TENSOR_TILES + VECTOR_TILES]
+            + [(t, a3_sum[t]) for t in GPSIMD_TILES]
+        )
+        with nc.allow_low_precision(reason="the sum is float32; its one rounding to bfloat16 is h's"):
+            for t in TENSOR_TILES + VECTOR_TILES + GPSIMD_TILES:
+                nc.vector.tensor_reduce(
+                    out=h_view[:, AGG_PASS, :, t],
+                    in_=a3_cols[t][:].rearrange("p (j n) -> p n j", j=J_CHUNK),
+                    axis=AXIS.X, op=ALU.add,
+                )
+        quantise_h(AGG_PASS)
+        node_layer(AGG_PASS, False, True)
+
+        out_rows = out.rearrange("b i g -> (b i) g")
+        half = WIDTH // 2
+        for i in range(WIDTH // half):
+            cols = slice(i * half, (i + 1) * half)
+            biased = work.tile([P, half], F32)
+            nc.vector.tensor_tensor(
+                out=biased[:], in0=out_ps[:, cols], in1=b0_all[:, cols], op=ALU.add
+            )
+            result = work.tile([P, half], F32)
+            nc.vector.scalar_tensor_tensor(
+                out=result[:], in0=biased[:], scalar=ALPHA, in1=biased[:],
+                op0=ALU.mult, op1=ALU.max,
+            )
+            nc.sync.dma_start(out=out_rows[:, cols], in_=result[:])

@@ -10,7 +10,6 @@ U8 = mybir.dt.uint8
 FP8X4 = mybir.dt.float8_e4m3fn_x4
 ALU = mybir.AluOpType
 ACT = mybir.ActivationFunctionType
-AXIS = mybir.AxisListType
 
 P = 128
 PACK = 4
@@ -26,26 +25,31 @@ CHUNKS = NEIGHBOURS // J_CHUNK
 COLS = J_CHUNK * NODES
 WORD_BLOCKS = K // 2 // P
 ALPHA = 0.2
-GPSIMD_TILES = (0, 1)
-TENSOR_TILES = (2,)
-VECTOR_TILES = (3,)
+TWO_SUMS, ONE_SUM = (3, 2), (0, 1)
+TENSOR_ADDS_TWO, TENSOR_ADDS_ONE = CHUNKS - 1, CHUNKS - 2
 PSUM_BANKS = 8
 AGG_PASS, X_PASS = 0, 1
+W0_PIECES = 4
+W0_PER_CHUNK = (0, 1, 1, 1, 1, 2, 2, 0)
 
 FLOPS = 2 * NODES * NEIGHBOURS * K * WIDTH + 2 * NODES * K * WIDTH
 
 
-def regroup(copy, raw, grouped, g):
+def regroup(copy, raw, grouped, g, first, count):
     copy(
-        out=grouped[g][:].rearrange("p (c i t) -> p c t i", i=4, t=PACK),
-        in_=raw[:, g * PACK : (g + 1) * PACK, :].rearrange("p t (c i) -> p c t i", i=4),
+        out=grouped[g][:, first * PACK : (first + count) * PACK].rearrange(
+            "p (c i t) -> p c t i", i=4, t=PACK
+        ),
+        in_=raw[:, g * PACK : (g + 1) * PACK, first : first + count].rearrange(
+            "p t (c i) -> p c t i", i=4
+        ),
     )
 
 
-def regroup_by_tile(copy, raw, grouped, g):
+def regroup_tile(copy, raw, grouped, g, i):
     copy(
-        out=grouped[g][:].rearrange("p (i m t) -> p i m t", i=F_TILES, t=PACK),
-        in_=raw[:, g * PACK : (g + 1) * PACK, :].rearrange("p t (m i) -> p i m t", i=F_TILES),
+        out=grouped[g][:, i * K_PASS : (i + 1) * K_PASS].rearrange("p (m t) -> p m t", t=PACK),
+        in_=raw[:, g * PACK : (g + 1) * PACK, :].rearrange("p t (m i) -> p i m t", i=F_TILES)[:, i],
     )
 
 
@@ -54,106 +58,59 @@ def tile_graph_gan_pb_kernel(tc, e2, x, fe_w2, fe_b2, fn_w0, fn_b0, out):
     with ExitStack() as stack:
         stack.enter_context(tc.manual_schedule())
         keep = stack.enter_context(tc.tile_pool(name="keep", bufs=1))
-        stage = stack.enter_context(tc.tile_pool(name="stage", bufs=3))
+        stage = stack.enter_context(tc.tile_pool(name="stage", bufs=4))
         work = stack.enter_context(tc.tile_pool(name="work", bufs=4))
-        psum_keep = stack.enter_context(tc.psum_pool(name="psum_keep", bufs=len(TENSOR_TILES)))
-        banks = stack.enter_context(
-            tc.psum_pool(name="banks", bufs=PSUM_BANKS - len(TENSOR_TILES))
-        )
+        banks = stack.enter_context(tc.psum_pool(name="banks", bufs=PSUM_BANKS))
 
         ident_f32 = keep.tile([P, P], F32)
         make_identity(nc, ident_f32[:])
 
-        x_sb = keep.tile([P, K_PASS], BF16)
-        nc.sync.dma_start(out=x_sb[:], in_=x.rearrange("b i d -> (b i) d"))
-        b2_raw = keep.tile([P, F_TILES], BF16)
-        nc.sync.dma_start(out=b2_raw[:], in_=fe_b2.rearrange("(p t) -> p t", p=P))
-        w1_raw = keep.tile([P, PASSES * PACK, WIDTH], BF16)
-        nc.sync.dma_start(
-            out=w1_raw[:].rearrange("p (g t) c -> p g t c", t=PACK),
-            in_=fe_w2.rearrange("(g p t) c -> p g t c", p=P, t=PACK),
-        )
         e2_rows = e2.rearrange("b i j k -> (b i) (j k)")
-        e2_sb = []
-        for c in range(CHUNKS):
-            e2_c = keep.tile([P, J_CHUNK * K], BF16, name="e2_%d" % c)
-            pieces = max(1, J_CHUNK >> c)
+        e2_sb = [
+            keep.tile([P, J_CHUNK * K], BF16, name="e2_%d" % c) for c in range(CHUNKS)
+        ]
+
+        def load_chunk(c, pieces):
             run = J_CHUNK * K // pieces
             for i in range(pieces):
                 first = c * J_CHUNK * K + i * run
                 nc.sync.dma_start(
-                    out=e2_c[:, i * run : (i + 1) * run], in_=e2_rows[:, first : first + run]
+                    out=e2_sb[c][:, i * run : (i + 1) * run], in_=e2_rows[:, first : first + run]
                 )
-            e2_sb.append(e2_c)
+
+        w1_raw = keep.tile([P, PASSES * PACK, WIDTH], BF16)
         w0_raw = keep.tile([P, PASSES * PACK, WIDTH], BF16)
-        nc.sync.dma_start(
-            out=w0_raw[:].rearrange("p (g t) c -> p g t c", t=PACK),
-            in_=fn_w0.rearrange("(g p t) c -> p g t c", p=P, t=PACK),
-        )
+
+        def load_weight(raw, weight, g):
+            nc.sync.dma_start(
+                out=raw[:, g * PACK : (g + 1) * PACK, :],
+                in_=weight[g * K_PASS : (g + 1) * K_PASS, :].rearrange(
+                    "(p t) c -> p t c", t=PACK
+                ),
+            )
+
+        b2_raw = keep.tile([P, F_TILES], BF16)
+        nc.sync.dma_start(out=b2_raw[:], in_=fe_b2.rearrange("(p t) -> p t", p=P))
+        load_chunk(0, J_CHUNK)
+        for g in range(PASSES):
+            load_weight(w1_raw, fe_w2, g)
+        x_sb = keep.tile([P, K_PASS], BF16)
+        nc.sync.dma_start(out=x_sb[:], in_=x.rearrange("b i d -> (b i) d"))
+        load_chunk(1, 2)
+        load_chunk(2, 2)
+        for g in range(PASSES):
+            load_weight(w0_raw, fn_w0, g)
+        for c in range(3, CHUNKS):
+            load_chunk(c, 1)
         b0_all = keep.tile([P, WIDTH], BF16)
         nc.sync.dma_start(out=b0_all[:], in_=fn_b0.partition_broadcast(P))
 
-        h_grouped = keep.tile([P, PASSES * NODES * PACK], BF16, align_bytes=64)
-        h_view = h_grouped[:].rearrange("p (g n t) -> p g n t", g=PASSES, t=PACK)
-        h_codes = keep.tile([P, PASSES, NODES], U32, align_bytes=64)
-        h_scales = keep.tile([P, PASSES, NODES], U8, align_bytes=64)
-
-        def quantise_h(g):
-            nc.vector.quantize_mx(
-                out=h_codes[:, g, :].bitcast(FP8X4),
-                scales=h_scales[:, g, :],
-                in_=h_grouped[:, g * NODES * PACK : (g + 1) * NODES * PACK],
-            )
-
-        x_words = x_sb[:].bitcast(F32)
-        x_ps = banks.tile([P, 2, NODES], F32, tag="bank")
-        for u in range(2):
-            nc.tensor.transpose(x_ps[:, u, :], x_words[:, u::2], ident_f32[:])
-        nc.vector.tensor_copy(
-            out=h_grouped[:].bitcast(F32).rearrange("p (g n u) -> p g n u", g=PASSES, u=2)[
-                :, X_PASS, :, :
-            ],
-            in_=x_ps[:].rearrange("p u n -> p n u"),
-        )
-        quantise_h(X_PASS)
-
-        b2 = keep.tile([P, F_TILES], F32)
-        nc.vector.tensor_copy(out=b2[:], in_=b2_raw[:])
-        b2_alpha = keep.tile([P, F_TILES], F32)
-        nc.vector.tensor_scalar_mul(out=b2_alpha[:], in0=b2[:], scalar1=ALPHA)
-        b2_neg = keep.tile([P, F_TILES], F32)
-        nc.vector.tensor_scalar_mul(out=b2_neg[:], in0=b2[:], scalar1=-1.0)
-        b2_column = keep.tile([P, F_TILES], F32)
-        nc.vector.tensor_scalar_mul(out=b2_column[:], in0=b2[:], scalar1=float(CHUNKS))
-
-        def weight_tiles(name):
-            grouped = [
-                keep.tile([P, WIDTH * PACK], BF16, align_bytes=64, name="%s_grouped_%d" % (name, g))
-                for g in range(PASSES)
-            ]
-            codes = keep.tile([P, PASSES, WIDTH], U32, align_bytes=64, name="%s_codes" % name)
-            scales = keep.tile([P, PASSES, WIDTH], U8, align_bytes=64, name="%s_scales" % name)
-            return grouped, codes, scales
-
-        def quantise_weight(grouped, codes, scales):
-            for g in range(PASSES):
-                nc.vector.quantize_mx(
-                    out=codes[:, g, :].bitcast(FP8X4), scales=scales[:, g, :], in_=grouped[g][:]
-                )
-
-        w1_grouped, w1_codes, w1_scales = weight_tiles("w1")
-        for g in range(PASSES):
-            regroup_by_tile(nc.vector.tensor_copy, w1_raw, w1_grouped, g)
-        quantise_weight(w1_grouped, w1_codes, w1_scales)
-        w0_grouped, w0_codes, w0_scales = weight_tiles("w0")
-
-        def quantise_chunk(c):
+        def transpose_half(c, half, grouped):
             e2_words = e2_sb[c][:].bitcast(F32)
-            grouped = stage.tile([P, PASSES * COLS * PACK], BF16, align_bytes=64)
             grouped_words = grouped[:].bitcast(F32).rearrange(
                 "p (g j n u) -> p g j n u", g=PASSES, j=J_CHUNK, u=2
             )
-            for j in range(J_CHUNK):
+            for j in range(half * J_CHUNK // 2, (half + 1) * J_CHUNK // 2):
                 xt = banks.tile([P, WORD_BLOCKS, NODES], F32, tag="bank")
                 for w in range(WORD_BLOCKS):
                     g, u = divmod(w, 2)
@@ -165,6 +122,12 @@ def tile_graph_gan_pb_kernel(tc, e2, x, fe_w2, fe_b2, fn_w0, fn_b0, out):
                     out=grouped_words[:, :, j, :, :],
                     in_=xt[:].rearrange("p (g u) n -> p g n u", u=2),
                 )
+
+        def new_grouped():
+            grouped = stage.tile([P, PASSES * COLS * PACK], BF16, align_bytes=64)
+            return grouped
+
+        def quantise_chunk(grouped):
             codes = stage.tile([P, PASSES, COLS], U32, align_bytes=64)
             scales = stage.tile([P, PASSES, COLS], U8, align_bytes=64)
             nc.vector.quantize_mx(
@@ -174,90 +137,194 @@ def tile_graph_gan_pb_kernel(tc, e2, x, fe_w2, fe_b2, fn_w0, fn_b0, out):
             )
             return codes, scales
 
-        a3_sum = dict((t, keep.tile([P, COLS], F32, name="a3_sum_%d" % t)) for t in GPSIMD_TILES)
-        clip_sum = dict(
-            (t, keep.tile([P, COLS], F32, name="clip_sum_%d" % t))
-            for t in TENSOR_TILES + VECTOR_TILES
-        )
-        line_sum = dict(
-            (t, keep.tile([P, COLS], F32, name="line_sum_%d" % t))
-            for t in TENSOR_TILES + VECTOR_TILES
-        )
-        v_sum = dict((t, psum_keep.tile([P, COLS], F32, name="v_sum_%d" % t)) for t in TENSOR_TILES)
+        def weight_tiles(name):
+            grouped = [
+                keep.tile([P, WIDTH * PACK], BF16, align_bytes=64, name="%s_grouped_%d" % (name, g))
+                for g in range(PASSES)
+            ]
+            codes = keep.tile([P, PASSES, WIDTH], U32, align_bytes=64, name="%s_codes" % name)
+            scales = keep.tile([P, PASSES, WIDTH], U8, align_bytes=64, name="%s_scales" % name)
+            return grouped, codes, scales
 
-        def edge_layer(c, codes, scales):
-            def multiply(bank, t, g, start, stop):
-                f_cols = slice(t * P, (t + 1) * P)
+        def quantise_weight(weight, g, first, count):
+            grouped, codes, scales = weight
+            nc.vector.quantize_mx(
+                out=codes[:, g, first : first + count].bitcast(FP8X4),
+                scales=scales[:, g, first : first + count],
+                in_=grouped[g][:, first * PACK : (first + count) * PACK],
+            )
+
+        w1 = weight_tiles("w1")
+        w0 = weight_tiles("w0")
+
+        h_grouped = keep.tile([P, PASSES * NODES * PACK], BF16, align_bytes=64)
+        h_codes = keep.tile([P, PASSES, NODES], U32, align_bytes=64)
+        h_scales = keep.tile([P, PASSES, NODES], U8, align_bytes=64)
+
+        def lay_h(turned, g):
+            nc.vector.tensor_copy(
+                out=h_grouped[:].bitcast(F32).rearrange("p (g n u) -> p g n u", g=PASSES, u=2)[
+                    :, g, :, :
+                ],
+                in_=turned[:].rearrange("p u n -> p n u"),
+            )
+
+        def quantise_h(g):
+            nc.vector.quantize_mx(
+                out=h_codes[:, g, :].bitcast(FP8X4),
+                scales=h_scales[:, g, :],
+                in_=h_grouped[:, g * NODES * PACK : (g + 1) * NODES * PACK],
+            )
+
+        b2 = keep.tile([P, F_TILES], F32)
+        b2_alpha = keep.tile([P, F_TILES], F32)
+        b2_neg = keep.tile([P, F_TILES], F32)
+        b2_rest = keep.tile([P, F_TILES], F32)
+
+        line_sum = {}
+        clip_sum = {}
+        late_a3 = []
+
+        def edge_tile(c, t, codes, scales):
+            acc = banks.tile([P, COLS], F32, tag="bank")
+            f_cols = slice(t * P, (t + 1) * P)
+            for g in range(PASSES):
                 nc.tensor.matmul_mx(
-                    out=bank[:],
-                    lhsT=w1_codes[:, g, f_cols].bitcast(FP8X4),
-                    lhsT_scale=w1_scales[:, g, f_cols],
+                    out=acc[:],
+                    lhsT=w1[1][:, g, f_cols].bitcast(FP8X4),
+                    lhsT_scale=w1[2][:, g, f_cols],
                     rhs=codes[:, g, :].bitcast(FP8X4),
                     rhs_scale=scales[:, g, :],
-                    start=start,
-                    stop=stop,
+                    start=g == 0,
+                    stop=g == PASSES - 1,
                 )
-
-            for t in range(F_TILES):
-                if t in TENSOR_TILES:
-                    for g in range(PASSES):
-                        multiply(
-                            v_sum[t], t, g, c == 0 and g == 0, c == CHUNKS - 1 and g == PASSES - 1
-                        )
-                acc = banks.tile([P, COLS], F32, tag="bank")
-                for g in range(PASSES):
-                    multiply(acc, t, g, g == 0, g == PASSES - 1)
-                if t in GPSIMD_TILES:
-                    scaled = work.tile([P, COLS], F32)
-                    nc.scalar.activation(
-                        out=scaled[:], in_=acc[:], func=ACT.Identity,
-                        bias=b2_alpha[:, t : t + 1], scale=ALPHA,
-                    )
-                    a3 = a3_sum[t] if c == 0 else work.tile([P, COLS], F32, name="a3")
-                    nc.vector.scalar_tensor_tensor(
-                        out=a3[:], in0=acc[:], scalar=b2[:, t : t + 1], in1=scaled[:],
-                        op0=ALU.add, op1=ALU.max,
-                    )
-                    if c > 0:
-                        nc.gpsimd.tensor_tensor(
-                            out=a3_sum[t][:], in0=a3_sum[t][:], in1=a3[:], op=ALU.add
-                        )
-                    continue
-                if t in VECTOR_TILES:
-                    if c == 0:
-                        nc.vector.tensor_scalar(
-                            out=line_sum[t][:], in0=acc[:], scalar1=ALPHA,
-                            scalar2=b2_column[:, t : t + 1], op0=ALU.mult, op1=ALU.add,
-                        )
-                    else:
-                        nc.vector.scalar_tensor_tensor(
-                            out=line_sum[t][:], in0=acc[:], scalar=ALPHA, in1=line_sum[t][:],
-                            op0=ALU.mult, op1=ALU.add,
-                        )
-                if c == 0:
-                    nc.vector.tensor_scalar_max(
-                        out=clip_sum[t][:], in0=acc[:], scalar1=b2_neg[:, t : t + 1]
+            tensor_adds = c >= (TENSOR_ADDS_TWO if t in TWO_SUMS else TENSOR_ADDS_ONE)
+            if t in TWO_SUMS and c > 0 and not tensor_adds:
+                nc.vector.scalar_tensor_tensor(
+                    out=line_sum[t][:], in0=acc[:], scalar=ALPHA, in1=line_sum[t][:],
+                    op0=ALU.mult, op1=ALU.add,
+                )
+                if c == 1:
+                    clip_sum[t] = keep.tile([P, COLS], F32, name="clip_sum_%d" % t)
+                    nc.vector.tensor_scalar(
+                        out=clip_sum[t][:], in0=acc[:], scalar1=b2_neg[:, t : t + 1],
+                        scalar2=b2_rest[:, t : t + 1], op0=ALU.max, op1=ALU.add,
                     )
                 else:
                     nc.vector.scalar_tensor_tensor(
                         out=clip_sum[t][:], in0=acc[:], scalar=b2_neg[:, t : t + 1],
                         in1=clip_sum[t][:], op0=ALU.max, op1=ALU.add,
                     )
-
-        ready = quantise_chunk(0)
-        for c in range(CHUNKS):
-            following = quantise_chunk(c + 1) if c + 1 < CHUNKS else None
-            edge_layer(c, ready[0], ready[1])
-            ready = following
-            g = c - (CHUNKS - PASSES)
-            if g >= 0:
-                regroup(nc.scalar.copy, w0_raw, w0_grouped, g)
-        for t in TENSOR_TILES:
+                return
+            scaled = work.tile([P, COLS], F32)
             nc.scalar.activation(
-                out=line_sum[t][:], in_=v_sum[t][:], func=ACT.Identity,
-                bias=b2_column[:, t : t + 1], scale=ALPHA,
+                out=scaled[:], in_=acc[:], func=ACT.Identity,
+                bias=b2_alpha[:, t : t + 1], scale=ALPHA,
             )
-        quantise_weight(w0_grouped, w0_codes, w0_scales)
+            if c == 0:
+                a3 = line_sum[t] = keep.tile([P, COLS], F32, name="line_sum_%d" % t)
+            elif tensor_adds:
+                a3 = keep.tile([P, COLS], F32, name="late_a3_%d_%d" % (c, t))
+                late_a3.append((t, a3))
+            else:
+                a3 = work.tile([P, COLS], F32, name="a3")
+            nc.vector.scalar_tensor_tensor(
+                out=a3[:], in0=acc[:], scalar=b2[:, t : t + 1], in1=scaled[:],
+                op0=ALU.add, op1=ALU.max,
+            )
+            if c > 0 and not tensor_adds:
+                nc.gpsimd.tensor_tensor(
+                    out=line_sum[t][:], in0=line_sum[t][:], in1=a3[:], op=ALU.add
+                )
+
+        agg_ps = {}
+
+        def word(pair):
+            return min(pair) // 2
+
+        def add_to_agg(t, columns, last=False):
+            pair = TWO_SUMS if t in TWO_SUMS else ONE_SUM
+            opens = pair not in agg_ps
+            if opens:
+                agg_bank = banks.tile([P, 2, P], F32, tag="bank")
+                agg_ps[pair] = agg_bank
+            for j in range(J_CHUNK):
+                nc.tensor.matmul(
+                    out=agg_ps[pair][:, t % 2, :],
+                    lhsT=columns[:, j * NODES : (j + 1) * NODES],
+                    rhs=ident_f32[:],
+                    start=opens and j == 0,
+                    stop=last and j == J_CHUNK - 1,
+                    is_transpose=True,
+                )
+
+        nc.vector.tensor_copy(out=b2[:], in_=b2_raw[:])
+        nc.vector.tensor_scalar_mul(out=b2_alpha[:], in0=b2[:], scalar1=ALPHA)
+        nc.vector.tensor_scalar_mul(out=b2_neg[:], in0=b2[:], scalar1=-1.0)
+        nc.vector.tensor_scalar_mul(
+            out=b2_rest[:], in0=b2[:], scalar1=(TENSOR_ADDS_TWO - 1) / (1.0 - ALPHA)
+        )
+        grouped = []
+        halves = []
+
+        def transpose_to(last_half):
+            for number in range(len(halves), last_half + 1):
+                c, half = divmod(number, 2)
+                if half == 0:
+                    grouped.append(new_grouped())
+                transpose_half(c, half, grouped[c])
+                halves.append(number)
+
+        transpose_to(1)
+        quantised = [quantise_chunk(grouped[0])]
+        for t in TWO_SUMS + ONE_SUM:
+            regroup_tile(nc.scalar.copy, w1_raw, w1[0], 0, t)
+        for t in TWO_SUMS + ONE_SUM:
+            quantise_weight(w1, 0, t * P, P)
+            regroup_tile(nc.vector.tensor_copy, w1_raw, w1[0], 1, t)
+            quantise_weight(w1, 1, t * P, P)
+
+        w0_pieces = [(g, i) for g in range(PASSES) for i in range(W0_PIECES)]
+        joined = {}
+        for c in range(CHUNKS):
+            if c == 0:
+                transpose_to(2)
+            elif c + 1 < CHUNKS:
+                transpose_to(2 * c + 3)
+            if c == 1:
+                quantised.append(quantise_chunk(grouped[1]))
+            if c == CHUNKS - 1:
+                for g in range(PASSES):
+                    quantise_weight(w0, g, 0, WIDTH)
+            codes, scales = quantised[c]
+            for t in TWO_SUMS:
+                edge_tile(c, t, codes, scales)
+            if 0 < c < CHUNKS - 1:
+                quantised.append(quantise_chunk(grouped[c + 1]))
+            for g, i in w0_pieces[: W0_PER_CHUNK[c]]:
+                columns = WIDTH // W0_PIECES
+                regroup(nc.scalar.copy, w0_raw, w0[0], g, i * columns, columns)
+            w0_pieces = w0_pieces[W0_PER_CHUNK[c] :]
+            if c == CHUNKS - 1:
+                for early in late_a3[: len(ONE_SUM)]:
+                    add_to_agg(*early)
+                late_a3 = late_a3[len(ONE_SUM) :]
+            for t in ONE_SUM:
+                edge_tile(c, t, codes, scales)
+            if c == 0:
+                x_words = x_sb[:].bitcast(F32)
+                turned = banks.tile([P, 2, NODES], F32, tag="bank")
+                for u in range(2):
+                    nc.tensor.transpose(turned[:, u, :], x_words[:, u::2], ident_f32[:])
+                lay_h(turned, X_PASS)
+                quantise_h(X_PASS)
+            if c == TENSOR_ADDS_TWO - 1:
+                for t in TWO_SUMS:
+                    joined[t] = keep.tile([P, COLS], F32, name="joined_%d" % t)
+                    nc.vector.scalar_tensor_tensor(
+                        out=joined[t][:], in0=clip_sum[t][:], scalar=1.0 - ALPHA,
+                        in1=line_sum[t][:], op0=ALU.mult, op1=ALU.add,
+                    )
 
         out_ps = banks.tile([P, WIDTH], F32, tag="bank")
 
@@ -266,33 +333,29 @@ def tile_graph_gan_pb_kernel(tc, e2, x, fe_w2, fe_b2, fn_w0, fn_b0, out):
                 out=out_ps[:],
                 lhsT=h_codes[:, g, :].bitcast(FP8X4),
                 lhsT_scale=h_scales[:, g, :],
-                rhs=w0_codes[:, g, :].bitcast(FP8X4),
-                rhs_scale=w0_scales[:, g, :],
+                rhs=w0[1][:, g, :].bitcast(FP8X4),
+                rhs_scale=w0[2][:, g, :],
                 start=start,
                 stop=stop,
             )
 
         node_layer(X_PASS, True, False)
-
-        def join_sums(t):
-            both = work.tile([P, COLS], F32)
-            nc.vector.scalar_tensor_tensor(
-                out=both[:], in0=clip_sum[t][:], scalar=1.0 - ALPHA, in1=line_sum[t][:],
-                op0=ALU.mult, op1=ALU.add,
+        for t in ONE_SUM:
+            add_to_agg(t, line_sum[t])
+        for t in TWO_SUMS:
+            add_to_agg(t, joined[t])
+        for t, a3 in late_a3:
+            add_to_agg(t, a3, last=t in (TWO_SUMS[-1], ONE_SUM[-1]))
+        agg_rows = keep.tile([P, 2, 2 * P], BF16)
+        for pair in (TWO_SUMS, ONE_SUM):
+            nc.vector.tensor_copy(
+                out=agg_rows[:, word(pair), :].rearrange("p (m i) -> p m i", i=2),
+                in_=agg_ps[pair][:].rearrange("p i m -> p m i"),
             )
-            return both
-
-        a3_cols = dict(
-            [(t, join_sums(t)) for t in TENSOR_TILES + VECTOR_TILES]
-            + [(t, a3_sum[t]) for t in GPSIMD_TILES]
-        )
-        with nc.allow_low_precision(reason="the sum is float32; its one rounding to bfloat16 is h's"):
-            for t in TENSOR_TILES + VECTOR_TILES + GPSIMD_TILES:
-                nc.vector.tensor_reduce(
-                    out=h_view[:, AGG_PASS, :, t],
-                    in_=a3_cols[t][:].rearrange("p (j n) -> p n j", j=J_CHUNK),
-                    axis=AXIS.X, op=ALU.add,
-                )
+        turned = banks.tile([P, 2, NODES], F32, tag="bank")
+        for u in (word(TWO_SUMS), word(ONE_SUM)):
+            nc.tensor.transpose(turned[:, u, :], agg_rows[:, u, :].bitcast(F32), ident_f32[:])
+        lay_h(turned, AGG_PASS)
         quantise_h(AGG_PASS)
         node_layer(AGG_PASS, False, True)
 

@@ -268,7 +268,7 @@ def tile_graph_gan_pb_kernel(tc, e2, x, fe_w2, fe_b2, fn_w0, fn_b0, out):
         halves = []
 
         def transpose_to(last_half):
-            for number in range(len(halves), last_half + 1):
+            for number in range(len(halves), min(last_half + 1, 2 * CHUNKS)):
                 c, half = divmod(number, 2)
                 if half == 0:
                     grouped.append(new_grouped())
@@ -287,19 +287,15 @@ def tile_graph_gan_pb_kernel(tc, e2, x, fe_w2, fe_b2, fn_w0, fn_b0, out):
         w0_pieces = [(g, i) for g in range(PASSES) for i in range(W0_PIECES)]
         joined = {}
         for c in range(CHUNKS):
-            if c == 0:
-                transpose_to(2)
-            elif c + 1 < CHUNKS:
-                transpose_to(2 * c + 3)
-            if c == 1:
-                quantised.append(quantise_chunk(grouped[1]))
+            transpose_to(2 if c == 0 else 2 * c + 3)
             if c == CHUNKS - 1:
                 for g in range(PASSES):
                     quantise_weight(w0, g, 0, WIDTH)
             codes, scales = quantised[c]
             for t in TWO_SUMS:
                 edge_tile(c, t, codes, scales)
-            if 0 < c < CHUNKS - 1:
+            transpose_to(3 if c == 0 else 2 * c + 4)
+            if c < CHUNKS - 1:
                 quantised.append(quantise_chunk(grouped[c + 1]))
             for g, i in w0_pieces[: W0_PER_CHUNK[c]]:
                 columns = WIDTH // W0_PIECES

@@ -26,11 +26,11 @@ COLS = J_CHUNK * NODES
 WORD_BLOCKS = K // 2 // P
 ALPHA = 0.2
 TWO_SUMS, ONE_SUM = (3, 2), (0, 1)
-TENSOR_ADDS_TWO, TENSOR_ADDS_ONE = CHUNKS - 1, CHUNKS - 2
+LATE = CHUNKS - 2
 PSUM_BANKS = 8
 AGG_PASS, X_PASS = 0, 1
 W0_PIECES = 4
-W0_PER_CHUNK = (0, 1, 1, 1, 1, 2, 2, 0)
+W0_PER_CHUNK = (0, 1, 1, 1, 2, 2, 1, 0)
 
 FLOPS = 2 * NODES * NEIGHBOURS * K * WIDTH + 2 * NODES * K * WIDTH
 
@@ -70,9 +70,9 @@ def tile_graph_gan_pb_kernel(tc, e2, x, fe_w2, fe_b2, fn_w0, fn_b0, out):
             keep.tile([P, J_CHUNK * K], BF16, name="e2_%d" % c) for c in range(CHUNKS)
         ]
 
-        def load_chunk(c, pieces):
+        def load_part(c, begin, end, pieces):
             run = J_CHUNK * K // pieces
-            for i in range(pieces):
+            for i in range(begin, end):
                 first = c * J_CHUNK * K + i * run
                 nc.sync.dma_start(
                     out=e2_sb[c][:, i * run : (i + 1) * run], in_=e2_rows[:, first : first + run]
@@ -91,17 +91,18 @@ def tile_graph_gan_pb_kernel(tc, e2, x, fe_w2, fe_b2, fn_w0, fn_b0, out):
 
         b2_raw = keep.tile([P, F_TILES], BF16)
         nc.sync.dma_start(out=b2_raw[:], in_=fe_b2.rearrange("(p t) -> p t", p=P))
-        load_chunk(0, J_CHUNK)
-        for g in range(PASSES):
-            load_weight(w1_raw, fe_w2, g)
+        load_part(0, 0, J_CHUNK, J_CHUNK)
+        load_weight(w1_raw, fe_w2, 0)
+        load_part(1, 0, 2, J_CHUNK)
+        load_weight(w1_raw, fe_w2, 1)
+        load_part(1, 2, J_CHUNK, J_CHUNK)
         x_sb = keep.tile([P, K_PASS], BF16)
         nc.sync.dma_start(out=x_sb[:], in_=x.rearrange("b i d -> (b i) d"))
-        load_chunk(1, 2)
-        load_chunk(2, 2)
+        load_part(2, 0, 2, 2)
         for g in range(PASSES):
             load_weight(w0_raw, fn_w0, g)
         for c in range(3, CHUNKS):
-            load_chunk(c, 1)
+            load_part(c, 0, 1, 1)
         b0_all = keep.tile([P, WIDTH], BF16)
         nc.sync.dma_start(out=b0_all[:], in_=fn_b0.partition_broadcast(P))
 
@@ -198,8 +199,7 @@ def tile_graph_gan_pb_kernel(tc, e2, x, fe_w2, fe_b2, fn_w0, fn_b0, out):
                     start=g == 0,
                     stop=g == PASSES - 1,
                 )
-            tensor_adds = c >= (TENSOR_ADDS_TWO if t in TWO_SUMS else TENSOR_ADDS_ONE)
-            if t in TWO_SUMS and c > 0 and not tensor_adds:
+            if t in TWO_SUMS and 0 < c < LATE:
                 nc.vector.scalar_tensor_tensor(
                     out=line_sum[t][:], in0=acc[:], scalar=ALPHA, in1=line_sum[t][:],
                     op0=ALU.mult, op1=ALU.add,
@@ -223,7 +223,7 @@ def tile_graph_gan_pb_kernel(tc, e2, x, fe_w2, fe_b2, fn_w0, fn_b0, out):
             )
             if c == 0:
                 a3 = line_sum[t] = keep.tile([P, COLS], F32, name="line_sum_%d" % t)
-            elif tensor_adds:
+            elif c >= LATE:
                 a3 = keep.tile([P, COLS], F32, name="late_a3_%d_%d" % (c, t))
                 late_a3.append((t, a3))
             else:
@@ -232,7 +232,7 @@ def tile_graph_gan_pb_kernel(tc, e2, x, fe_w2, fe_b2, fn_w0, fn_b0, out):
                 out=a3[:], in0=acc[:], scalar=b2[:, t : t + 1], in1=scaled[:],
                 op0=ALU.add, op1=ALU.max,
             )
-            if c > 0 and not tensor_adds:
+            if 0 < c < LATE:
                 nc.gpsimd.tensor_tensor(
                     out=line_sum[t][:], in0=line_sum[t][:], in1=a3[:], op=ALU.add
                 )
@@ -262,7 +262,7 @@ def tile_graph_gan_pb_kernel(tc, e2, x, fe_w2, fe_b2, fn_w0, fn_b0, out):
         nc.vector.tensor_scalar_mul(out=b2_alpha[:], in0=b2[:], scalar1=ALPHA)
         nc.vector.tensor_scalar_mul(out=b2_neg[:], in0=b2[:], scalar1=-1.0)
         nc.vector.tensor_scalar_mul(
-            out=b2_rest[:], in0=b2[:], scalar1=(TENSOR_ADDS_TWO - 1) / (1.0 - ALPHA)
+            out=b2_rest[:], in0=b2[:], scalar1=(LATE - 1) / (1.0 - ALPHA)
         )
         grouped = []
         halves = []
@@ -289,8 +289,18 @@ def tile_graph_gan_pb_kernel(tc, e2, x, fe_w2, fe_b2, fn_w0, fn_b0, out):
         for c in range(CHUNKS):
             transpose_to(2 if c == 0 else 2 * c + 3)
             if c == CHUNKS - 1:
+                for t in TWO_SUMS:
+                    joined[t] = keep.tile([P, COLS], F32, name="joined_%d" % t)
+                    nc.vector.scalar_tensor_tensor(
+                        out=joined[t][:], in0=clip_sum[t][:], scalar=1.0 - ALPHA,
+                        in1=line_sum[t][:], op0=ALU.mult, op1=ALU.add,
+                    )
                 for g in range(PASSES):
                     quantise_weight(w0, g, 0, WIDTH)
+                for t, a3 in late_a3[: len(TWO_SUMS)]:
+                    add_to_agg(t, a3)
+                for t in ONE_SUM:
+                    add_to_agg(t, line_sum[t])
             codes, scales = quantised[c]
             for t in TWO_SUMS:
                 edge_tile(c, t, codes, scales)
@@ -302,9 +312,8 @@ def tile_graph_gan_pb_kernel(tc, e2, x, fe_w2, fe_b2, fn_w0, fn_b0, out):
                 regroup(nc.scalar.copy, w0_raw, w0[0], g, i * columns, columns)
             w0_pieces = w0_pieces[W0_PER_CHUNK[c] :]
             if c == CHUNKS - 1:
-                for early in late_a3[: len(ONE_SUM)]:
-                    add_to_agg(*early)
-                late_a3 = late_a3[len(ONE_SUM) :]
+                for t, a3 in late_a3[len(TWO_SUMS) : F_TILES]:
+                    add_to_agg(t, a3)
             for t in ONE_SUM:
                 edge_tile(c, t, codes, scales)
             if c == 0:
@@ -314,13 +323,6 @@ def tile_graph_gan_pb_kernel(tc, e2, x, fe_w2, fe_b2, fn_w0, fn_b0, out):
                     nc.tensor.transpose(turned[:, u, :], x_words[:, u::2], ident_f32[:])
                 lay_h(turned, X_PASS)
                 quantise_h(X_PASS)
-            if c == TENSOR_ADDS_TWO - 1:
-                for t in TWO_SUMS:
-                    joined[t] = keep.tile([P, COLS], F32, name="joined_%d" % t)
-                    nc.vector.scalar_tensor_tensor(
-                        out=joined[t][:], in0=clip_sum[t][:], scalar=1.0 - ALPHA,
-                        in1=line_sum[t][:], op0=ALU.mult, op1=ALU.add,
-                    )
 
         out_ps = banks.tile([P, WIDTH], F32, tag="bank")
 
@@ -336,11 +338,9 @@ def tile_graph_gan_pb_kernel(tc, e2, x, fe_w2, fe_b2, fn_w0, fn_b0, out):
             )
 
         node_layer(X_PASS, True, False)
-        for t in ONE_SUM:
-            add_to_agg(t, line_sum[t])
         for t in TWO_SUMS:
             add_to_agg(t, joined[t])
-        for t, a3 in late_a3:
+        for t, a3 in late_a3[F_TILES:]:
             add_to_agg(t, a3, last=t in (TWO_SUMS[-1], ONE_SUM[-1]))
         agg_rows = keep.tile([P, 2, 2 * P], BF16)
         for pair in (TWO_SUMS, ONE_SUM):

@@ -26,6 +26,7 @@ COLS = J_CHUNK * NODES
 WORD_BLOCKS = K // 2 // P
 ALPHA = 0.2
 TWO_SUMS, ONE_SUM = (3, 2), (0, 1)
+WARM_UPS = 3
 LATE = CHUNKS - 2
 PSUM_BANKS = 8
 AGG_PASS, X_PASS = 0, 1
@@ -276,6 +277,11 @@ def tile_graph_gan_pb_kernel(tc, e2, x, fe_w2, fe_b2, fn_w0, fn_b0, out):
                 halves.append(number)
 
         transpose_to(1)
+        warm_up = banks.tile([P, COLS], F32, tag="bank")
+        for _ in range(WARM_UPS):
+            nc.tensor.matmul(
+                out=warm_up[:], lhsT=e2_sb[0][:, 0:P], rhs=e2_sb[0][:, 0:COLS], start=True, stop=True
+            )
         quantised = [quantise_chunk(grouped[0])]
         for t in TWO_SUMS + ONE_SUM:
             regroup_tile(nc.scalar.copy, w1_raw, w1[0], 0, t)

@@ -26,12 +26,13 @@ COLS = J_CHUNK * NODES
 WORD_BLOCKS = K // 2 // P
 ALPHA = 0.2
 TWO_SUMS, ONE_SUM = (3, 2), (0, 1)
-WARM_UPS = 3
+WARM_UPS = 4
 LATE = CHUNKS - 2
 PSUM_BANKS = 8
 AGG_PASS, X_PASS = 0, 1
 W0_PIECES = 4
-W0_PER_CHUNK = (0, 1, 1, 1, 2, 2, 1, 0)
+W0_PER_CHUNK = (0, 1, 1, 1, 1, 2, 2, 0)
+W0_FIRST_PASS = 5
 
 FLOPS = 2 * NODES * NEIGHBOURS * K * WIDTH + 2 * NODES * K * WIDTH
 
@@ -301,8 +302,7 @@ def tile_graph_gan_pb_kernel(tc, e2, x, fe_w2, fe_b2, fn_w0, fn_b0, out):
                         out=joined[t][:], in0=clip_sum[t][:], scalar=1.0 - ALPHA,
                         in1=line_sum[t][:], op0=ALU.mult, op1=ALU.add,
                     )
-                for g in range(PASSES):
-                    quantise_weight(w0, g, 0, WIDTH)
+                quantise_weight(w0, 1, 0, WIDTH)
                 for t, a3 in late_a3[: len(TWO_SUMS)]:
                     add_to_agg(t, a3)
                 for t in ONE_SUM:
@@ -311,6 +311,8 @@ def tile_graph_gan_pb_kernel(tc, e2, x, fe_w2, fe_b2, fn_w0, fn_b0, out):
             for t in TWO_SUMS:
                 edge_tile(c, t, codes, scales)
             transpose_to(3 if c == 0 else 2 * c + 4)
+            if c == W0_FIRST_PASS:
+                quantise_weight(w0, 0, 0, WIDTH)
             if c < CHUNKS - 1:
                 quantised.append(quantise_chunk(grouped[c + 1]))
             for g, i in w0_pieces[: W0_PER_CHUNK[c]]:

@@ -27,7 +27,7 @@ WORD_BLOCKS = K // 2 // P
 ALPHA = 0.2
 TWO_SUMS, ONE_SUM = (3, 2), (0, 1)
 WARM_UPS = 4
-LATE = CHUNKS - 2
+LATE = {0: CHUNKS - 2, 1: CHUNKS - 2, 2: CHUNKS - 2, 3: CHUNKS - 1}
 PSUM_BANKS = 8
 AGG_PASS, X_PASS = 0, 1
 W0_PIECES = 4
@@ -101,9 +101,10 @@ def tile_graph_gan_pb_kernel(tc, e2, x, fe_w2, fe_b2, fn_w0, fn_b0, out):
         x_sb = keep.tile([P, K_PASS], BF16)
         nc.sync.dma_start(out=x_sb[:], in_=x.rearrange("b i d -> (b i) d"))
         load_part(2, 0, 2, 2)
-        for g in range(PASSES):
-            load_weight(w0_raw, fn_w0, g)
-        for c in range(3, CHUNKS):
+        load_weight(w0_raw, fn_w0, 0)
+        load_part(3, 0, 2, 2)
+        load_weight(w0_raw, fn_w0, 1)
+        for c in range(4, CHUNKS):
             load_part(c, 0, 1, 1)
         b0_all = keep.tile([P, WIDTH], BF16)
         nc.sync.dma_start(out=b0_all[:], in_=fn_b0.partition_broadcast(P))
@@ -201,7 +202,7 @@ def tile_graph_gan_pb_kernel(tc, e2, x, fe_w2, fe_b2, fn_w0, fn_b0, out):
                     start=g == 0,
                     stop=g == PASSES - 1,
                 )
-            if t in TWO_SUMS and 0 < c < LATE:
+            if t in TWO_SUMS and 0 < c < LATE[t]:
                 nc.vector.scalar_tensor_tensor(
                     out=line_sum[t][:], in0=acc[:], scalar=ALPHA, in1=line_sum[t][:],
                     op0=ALU.mult, op1=ALU.add,
@@ -225,7 +226,7 @@ def tile_graph_gan_pb_kernel(tc, e2, x, fe_w2, fe_b2, fn_w0, fn_b0, out):
             )
             if c == 0:
                 a3 = line_sum[t] = keep.tile([P, COLS], F32, name="line_sum_%d" % t)
-            elif c >= LATE:
+            elif c >= LATE[t]:
                 a3 = keep.tile([P, COLS], F32, name="late_a3_%d_%d" % (c, t))
                 late_a3.append((t, a3))
             else:
@@ -234,7 +235,7 @@ def tile_graph_gan_pb_kernel(tc, e2, x, fe_w2, fe_b2, fn_w0, fn_b0, out):
                 out=a3[:], in0=acc[:], scalar=b2[:, t : t + 1], in1=scaled[:],
                 op0=ALU.add, op1=ALU.max,
             )
-            if 0 < c < LATE:
+            if 0 < c < LATE[t]:
                 nc.gpsimd.tensor_tensor(
                     out=line_sum[t][:], in0=line_sum[t][:], in1=a3[:], op=ALU.add
                 )
@@ -263,9 +264,11 @@ def tile_graph_gan_pb_kernel(tc, e2, x, fe_w2, fe_b2, fn_w0, fn_b0, out):
         nc.vector.tensor_copy(out=b2[:], in_=b2_raw[:])
         nc.vector.tensor_scalar_mul(out=b2_alpha[:], in0=b2[:], scalar1=ALPHA)
         nc.vector.tensor_scalar_mul(out=b2_neg[:], in0=b2[:], scalar1=-1.0)
-        nc.vector.tensor_scalar_mul(
-            out=b2_rest[:], in0=b2[:], scalar1=(LATE - 1) / (1.0 - ALPHA)
-        )
+        for t in TWO_SUMS:
+            nc.vector.tensor_scalar_mul(
+                out=b2_rest[:, t : t + 1], in0=b2[:, t : t + 1],
+                scalar1=(LATE[t] - 1) / (1.0 - ALPHA),
+            )
         grouped = []
         halves = []
 
@@ -303,7 +306,7 @@ def tile_graph_gan_pb_kernel(tc, e2, x, fe_w2, fe_b2, fn_w0, fn_b0, out):
                         in1=line_sum[t][:], op0=ALU.mult, op1=ALU.add,
                     )
                 quantise_weight(w0, 1, 0, WIDTH)
-                for t, a3 in late_a3[: len(TWO_SUMS)]:
+                for t, a3 in late_a3[:1]:
                     add_to_agg(t, a3)
                 for t in ONE_SUM:
                     add_to_agg(t, line_sum[t])
@@ -320,7 +323,7 @@ def tile_graph_gan_pb_kernel(tc, e2, x, fe_w2, fe_b2, fn_w0, fn_b0, out):
                 regroup(nc.scalar.copy, w0_raw, w0[0], g, i * columns, columns)
             w0_pieces = w0_pieces[W0_PER_CHUNK[c] :]
             if c == CHUNKS - 1:
-                for t, a3 in late_a3[len(TWO_SUMS) : F_TILES]:
+                for t, a3 in late_a3[1:3]:
                     add_to_agg(t, a3)
             for t in ONE_SUM:
                 edge_tile(c, t, codes, scales)
@@ -348,7 +351,7 @@ def tile_graph_gan_pb_kernel(tc, e2, x, fe_w2, fe_b2, fn_w0, fn_b0, out):
         node_layer(X_PASS, True, False)
         for t in TWO_SUMS:
             add_to_agg(t, joined[t])
-        for t, a3 in late_a3[F_TILES:]:
+        for t, a3 in late_a3[3:]:
             add_to_agg(t, a3, last=t in (TWO_SUMS[-1], ONE_SUM[-1]))
         agg_rows = keep.tile([P, 2, 2 * P], BF16)
         for pair in (TWO_SUMS, ONE_SUM):

from contextlib import ExitStack

import concourse.mybir as mybir
from concourse.masks import make_identity

F32 = mybir.dt.float32
BF16 = mybir.dt.bfloat16
U32 = mybir.dt.uint32
U8 = mybir.dt.uint8
FP8X4 = mybir.dt.float8_e4m3fn_x4
ALU = mybir.AluOpType
ACT = mybir.ActivationFunctionType

P = 128
PACK = 4
K_PASS = P * PACK
NODES = 128
NEIGHBOURS = 32
K = 1024
PASSES = K // K_PASS
WIDTH = 512
F_TILES = WIDTH // P
J_CHUNK = 4
CHUNKS = NEIGHBOURS // J_CHUNK
COLS = J_CHUNK * NODES
WORD_BLOCKS = K // 2 // P
ALPHA = 0.2
TWO_SUMS, ONE_SUM = (3, 2), (0, 1)
WARM_UPS = 4
LATE = {0: CHUNKS - 2, 1: CHUNKS - 2, 2: CHUNKS - 2, 3: CHUNKS - 1}
PSUM_BANKS = 8
AGG_PASS, X_PASS = 0, 1
W0_PIECES = 4
W0_PER_CHUNK = (0, 1, 1, 1, 1, 2, 2, 0)
W0_FIRST_PASS = 5

FLOPS = 2 * NODES * NEIGHBOURS * K * WIDTH + 2 * NODES * K * WIDTH


def regroup(copy, raw, grouped, g, first, count):
    copy(
        out=grouped[g][:, first * PACK : (first + count) * PACK].rearrange(
            "p (c i t) -> p c t i", i=4, t=PACK
        ),
        in_=raw[:, g * PACK : (g + 1) * PACK, first : first + count].rearrange(
            "p t (c i) -> p c t i", i=4
        ),
    )


def regroup_tile(copy, raw, grouped, g, i):
    copy(
        out=grouped[g][:, i * K_PASS : (i + 1) * K_PASS].rearrange("p (m t) -> p m t", t=PACK),
        in_=raw[:, g * PACK : (g + 1) * PACK, :].rearrange("p t (m i) -> p i m t", i=F_TILES)[:, i],
    )


def tile_graph_gan_pb_kernel(tc, e2, x, fe_w2, fe_b2, fn_w0, fn_b0, out):
    nc = tc.nc
    with ExitStack() as stack:
        stack.enter_context(tc.manual_schedule())
        keep = stack.enter_context(tc.tile_pool(name="keep", bufs=1))
        stage = stack.enter_context(tc.tile_pool(name="stage", bufs=4))
        work = stack.enter_context(tc.tile_pool(name="work", bufs=4))
        banks = stack.enter_context(tc.psum_pool(name="banks", bufs=PSUM_BANKS))

        ident_f32 = keep.tile([P, P], F32)
        make_identity(nc, ident_f32[:])

        e2_rows = e2.rearrange("b i j k -> (b i) (j k)")
        e2_sb = [
            keep.tile([P, J_CHUNK * K], BF16, name="e2_%d" % c) for c in range(CHUNKS)
        ]

        def load_part(c, begin, end, pieces):
            run = J_CHUNK * K // pieces
            for i in range(begin, end):
                first = c * J_CHUNK * K + i * run
                nc.sync.dma_start(
                    out=e2_sb[c][:, i * run : (i + 1) * run], in_=e2_rows[:, first : first + run]
                )

        w1_raw = keep.tile([P, PASSES * PACK, WIDTH], BF16)
        w0_raw = keep.tile([P, PASSES * PACK, WIDTH], BF16)

        def load_weight(raw, weight, g):
            nc.sync.dma_start(
                out=raw[:, g * PACK : (g + 1) * PACK, :],
                in_=weight[g * K_PASS : (g + 1) * K_PASS, :].rearrange(
                    "(p t) c -> p t c", t=PACK
                ),
            )

        b2_raw = keep.tile([P, F_TILES], BF16)
        nc.sync.dma_start(out=b2_raw[:], in_=fe_b2.rearrange("(p t) -> p t", p=P))
        load_part(0, 0, J_CHUNK, J_CHUNK)
        load_weight(w1_raw, fe_w2, 0)
        load_part(1, 0, 2, J_CHUNK)
        load_weight(w1_raw, fe_w2, 1)
        load_part(1, 2, J_CHUNK, J_CHUNK)
        x_sb = keep.tile([P, K_PASS], BF16)
        nc.sync.dma_start(out=x_sb[:], in_=x.rearrange("b i d -> (b i) d"))
        load_part(2, 0, 2, 2)
        load_weight(w0_raw, fn_w0, 0)
        load_part(3, 0, 2, 2)
        load_weight(w0_raw, fn_w0, 1)
        for c in range(4, CHUNKS):
            load_part(c, 0, 1, 1)
        b0_all = keep.tile([P, WIDTH], BF16)
        nc.sync.dma_start(out=b0_all[:], in_=fn_b0.partition_broadcast(P))

        def transpose_half(c, half, grouped):
            e2_words = e2_sb[c][:].bitcast(F32)
            grouped_words = grouped[:].bitcast(F32).rearrange(
                "p (g j n u) -> p g j n u", g=PASSES, j=J_CHUNK, u=2
            )
            for j in range(half * J_CHUNK // 2, (half + 1) * J_CHUNK // 2):
                xt = banks.tile([P, WORD_BLOCKS, NODES], F32, tag="bank")
                for w in range(WORD_BLOCKS):
                    g, u = divmod(w, 2)
                    first = (j * PASSES + g) * 2 * P
                    nc.tensor.transpose(
                        xt[:, w, :], e2_words[:, first + u : first + 2 * P : 2], ident_f32[:]
                    )
                nc.scalar.copy(
                    out=grouped_words[:, :, j, :, :],
                    in_=xt[:].rearrange("p (g u) n -> p g n u", u=2),
                )

        def new_grouped():
            grouped = stage.tile([P, PASSES * COLS * PACK], BF16, align_bytes=64)
            return grouped

        def quantise_chunk(grouped):
            codes = stage.tile([P, PASSES, COLS], U32, align_bytes=64)
            scales = stage.tile([P, PASSES, COLS], U8, align_bytes=64)
            nc.vector.quantize_mx(
                out=codes[:].rearrange("p g c -> p (g c)").bitcast(FP8X4),
                scales=scales[:].rearrange("p g c -> p (g c)"),
                in_=grouped[:],
            )
            return codes, scales

        def weight_tiles(name):
            grouped = [
                keep.tile([P, WIDTH * PACK], BF16, align_bytes=64, name="%s_grouped_%d" % (name, g))
                for g in range(PASSES)
            ]
            codes = keep.tile([P, PASSES, WIDTH], U32, align_bytes=64, name="%s_codes" % name)
            scales = keep.tile([P, PASSES, WIDTH], U8, align_bytes=64, name="%s_scales" % name)
            return grouped, codes, scales

        def quantise_weight(weight, g, first, count):
            grouped, codes, scales = weight
            nc.vector.quantize_mx(
                out=codes[:, g, first : first + count].bitcast(FP8X4),
                scales=scales[:, g, first : first + count],
                in_=grouped[g][:, first * PACK : (first + count) * PACK],
            )

        w1 = weight_tiles("w1")
        w0 = weight_tiles("w0")

        h_grouped = keep.tile([P, PASSES * NODES * PACK], BF16, align_bytes=64)
        h_codes = keep.tile([P, PASSES, NODES], U32, align_bytes=64)
        h_scales = keep.tile([P, PASSES, NODES], U8, align_bytes=64)

        def lay_h(turned, g):
            nc.vector.tensor_copy(
                out=h_grouped[:].bitcast(F32).rearrange("p (g n u) -> p g n u", g=PASSES, u=2)[
                    :, g, :, :
                ],
                in_=turned[:].rearrange("p u n -> p n u"),
            )

        def quantise_h(g):
            nc.vector.quantize_mx(
                out=h_codes[:, g, :].bitcast(FP8X4),
                scales=h_scales[:, g, :],
                in_=h_grouped[:, g * NODES * PACK : (g + 1) * NODES * PACK],
            )

        b2 = keep.tile([P, F_TILES], F32)
        b2_alpha = keep.tile([P, F_TILES], F32)
        b2_neg = keep.tile([P, F_TILES], F32)
        b2_rest = keep.tile([P, F_TILES], F32)

        line_sum = {}
        clip_sum = {}
        late_a3 = []

        def edge_tile(c, t, codes, scales):
            acc = banks.tile([P, COLS], F32, tag="bank")
            f_cols = slice(t * P, (t + 1) * P)
            for g in range(PASSES):
                nc.tensor.matmul_mx(
                    out=acc[:],
                    lhsT=w1[1][:, g, f_cols].bitcast(FP8X4),
                    lhsT_scale=w1[2][:, g, f_cols],
                    rhs=codes[:, g, :].bitcast(FP8X4),
                    rhs_scale=scales[:, g, :],
                    start=g == 0,
                    stop=g == PASSES - 1,
                )
            if t in TWO_SUMS and 0 < c < LATE[t]:
                nc.vector.scalar_tensor_tensor(
                    out=line_sum[t][:], in0=acc[:], scalar=ALPHA, in1=line_sum[t][:],
                    op0=ALU.mult, op1=ALU.add,
                )
                if c == 1:
                    clip_sum[t] = keep.tile([P, COLS], F32, name="clip_sum_%d" % t)
                    nc.vector.tensor_scalar(
                        out=clip_sum[t][:], in0=acc[:], scalar1=b2_neg[:, t : t + 1],
                        scalar2=b2_rest[:, t : t + 1], op0=ALU.max, op1=ALU.add,
                    )
                else:
                    nc.vector.scalar_tensor_tensor(
                        out=clip_sum[t][:], in0=acc[:], scalar=b2_neg[:, t : t + 1],
                        in1=clip_sum[t][:], op0=ALU.max, op1=ALU.add,
                    )
                return
            scaled = work.tile([P, COLS], F32)
            nc.scalar.activation(
                out=scaled[:], in_=acc[:], func=ACT.Identity,
                bias=b2_alpha[:, t : t + 1], scale=ALPHA,
            )
            if c == 0:
                a3 = line_sum[t] = keep.tile([P, COLS], F32, name="line_sum_%d" % t)
            elif c >= LATE[t]:
                a3 = keep.tile([P, COLS], F32, name="late_a3_%d_%d" % (c, t))
                late_a3.append((t, a3))
            else:
                a3 = work.tile([P, COLS], F32, name="a3")
            nc.vector.scalar_tensor_tensor(
                out=a3[:], in0=acc[:], scalar=b2[:, t : t + 1], in1=scaled[:],
                op0=ALU.add, op1=ALU.max,
            )
            if 0 < c < LATE[t]:
                nc.gpsimd.tensor_tensor(
                    out=line_sum[t][:], in0=line_sum[t][:], in1=a3[:], op=ALU.add
                )

        agg_ps = {}

        def word(pair):
            return min(pair) // 2

        def add_to_agg(t, columns, last=False):
            pair = TWO_SUMS if t in TWO_SUMS else ONE_SUM
            opens = pair not in agg_ps
            if opens:
                agg_bank = banks.tile([P, 2, P], F32, tag="bank")
                agg_ps[pair] = agg_bank
            for j in range(J_CHUNK):
                nc.tensor.matmul(
                    out=agg_ps[pair][:, t % 2, :],
                    lhsT=columns[:, j * NODES : (j + 1) * NODES],
                    rhs=ident_f32[:],
                    start=opens and j == 0,
                    stop=last and j == J_CHUNK - 1,
                    is_transpose=True,
                )

        nc.vector.tensor_copy(out=b2[:], in_=b2_raw[:])
        nc.vector.tensor_scalar_mul(out=b2_alpha[:], in0=b2[:], scalar1=ALPHA)
        nc.vector.tensor_scalar_mul(out=b2_neg[:], in0=b2[:], scalar1=-1.0)
        for t in TWO_SUMS:
            nc.vector.tensor_scalar_mul(
                out=b2_rest[:, t : t + 1], in0=b2[:, t : t + 1],
                scalar1=(LATE[t] - 1) / (1.0 - ALPHA),
            )
        grouped = []
        halves = []

        def transpose_to(last_half):
            for number in range(len(halves), min(last_half + 1, 2 * CHUNKS)):
                c, half = divmod(number, 2)
                if half == 0:
                    grouped.append(new_grouped())
                transpose_half(c, half, grouped[c])
                halves.append(number)

        transpose_to(1)
        warm_up = banks.tile([P, COLS], F32, tag="bank")
        for _ in range(WARM_UPS):
            nc.tensor.matmul(
                out=warm_up[:], lhsT=e2_sb[0][:, 0:P], rhs=e2_sb[0][:, 0:COLS], start=True, stop=True
            )
        quantised = [quantise_chunk(grouped[0])]
        for t in TWO_SUMS + ONE_SUM:
            regroup_tile(nc.scalar.copy, w1_raw, w1[0], 0, t)
        for t in TWO_SUMS + ONE_SUM:
            quantise_weight(w1, 0, t * P, P)
            regroup_tile(nc.vector.tensor_copy, w1_raw, w1[0], 1, t)
            quantise_weight(w1, 1, t * P, P)

        w0_pieces = [(g, i) for g in range(PASSES) for i in range(W0_PIECES)]
        joined = {}
        for c in range(CHUNKS):
            transpose_to(2 if c == 0 else 2 * c + 3)
            if c == CHUNKS - 1:
                for t in TWO_SUMS:
                    joined[t] = keep.tile([P, COLS], F32, name="joined_%d" % t)
                    nc.vector.scalar_tensor_tensor(
                        out=joined[t][:], in0=clip_sum[t][:], scalar=1.0 - ALPHA,
                        in1=line_sum[t][:], op0=ALU.mult, op1=ALU.add,
                    )
                quantise_weight(w0, 1, 0, WIDTH)
                for t, a3 in late_a3[:1]:
                    add_to_agg(t, a3)
                for t in ONE_SUM:
                    add_to_agg(t, line_sum[t])
            codes, scales = quantised[c]
            for t in TWO_SUMS:
                edge_tile(c, t, codes, scales)
            transpose_to(3 if c == 0 else 2 * c + 4)
            if c == W0_FIRST_PASS:
                quantise_weight(w0, 0, 0, WIDTH)
            if c < CHUNKS - 1:
                quantised.append(quantise_chunk(grouped[c + 1]))
            for g, i in w0_pieces[: W0_PER_CHUNK[c]]:
                columns = WIDTH // W0_PIECES
                regroup(nc.scalar.copy, w0_raw, w0[0], g, i * columns, columns)
            w0_pieces = w0_pieces[W0_PER_CHUNK[c] :]
            if c == CHUNKS - 1:
                for t, a3 in late_a3[1:3]:
                    add_to_agg(t, a3)
            for t in ONE_SUM:
                edge_tile(c, t, codes, scales)
            if c == 0:
                x_words = x_sb[:].bitcast(F32)
                turned = banks.tile([P, 2, NODES], F32, tag="bank")
                for u in range(2):
                    nc.tensor.transpose(turned[:, u, :], x_words[:, u::2], ident_f32[:])
                lay_h(turned, X_PASS)
                quantise_h(X_PASS)

        out_ps = banks.tile([P, WIDTH], F32, tag="bank")

        def node_layer(g, start, stop):
            nc.tensor.matmul_mx(
                out=out_ps[:],
                lhsT=h_codes[:, g, :].bitcast(FP8X4),
                lhsT_scale=h_scales[:, g, :],
                rhs=w0[1][:, g, :].bitcast(FP8X4),
                rhs_scale=w0[2][:, g, :],
                start=start,
                stop=stop,
            )

        node_layer(X_PASS, True, False)
        for t in TWO_SUMS:
            add_to_agg(t, joined[t])
        for t, a3 in late_a3[3:]:
            add_to_agg(t, a3, last=t in (TWO_SUMS[-1], ONE_SUM[-1]))
        agg_rows = keep.tile([P, 2, 2 * P], BF16)
        for pair in (TWO_SUMS, ONE_SUM):
            nc.vector.tensor_copy(
                out=agg_rows[:, word(pair), :].rearrange("p (m i) -> p m i", i=2),
                in_=agg_ps[pair][:].rearrange("p i m -> p m i"),
            )
        turned = banks.tile([P, 2, NODES], F32, tag="bank")
        for u in (word(TWO_SUMS), word(ONE_SUM)):
            nc.tensor.transpose(turned[:, u, :], agg_rows[:, u, :].bitcast(F32), ident_f32[:])
        lay_h(turned, AGG_PASS)
        quantise_h(AGG_PASS)
        node_layer(AGG_PASS, False, True)

        out_rows = out.rearrange("b i g -> (b i) g")
        half = WIDTH // 2
        for i in range(WIDTH // half):
            cols = slice(i * half, (i + 1) * half)
            biased = work.tile([P, half], F32)
            nc.vector.tensor_tensor(
                out=biased[:], in0=out_ps[:, cols], in1=b0_all[:, cols], op=ALU.add
            )
            result = work.tile([P, half], F32)
            nc.vector.scalar_tensor_tensor(
                out=result[:], in0=biased[:], scalar=ALPHA, in1=biased[:],
                op0=ALU.mult, op1=ALU.max,
            )
            nc.sync.dma_start(out=out_rows[:, cols], in_=result[:])
